import numpy as np
import ml_dtypes


def mxq(x, axis, fmt="e4m3"):
    dtype, down = {"e4m3": (ml_dtypes.float8_e4m3fn, 7), "e5m2": (ml_dtypes.float8_e5m2, 14)}[fmt]
    v = np.moveaxis(np.asarray(x, np.float32).astype(ml_dtypes.bfloat16).astype(np.float64), axis, -1)
    blocks = v.reshape(v.shape[:-1] + (-1, 32))
    amax = np.abs(blocks).max(-1, keepdims=True)
    byte = np.maximum(np.where(amax > 0, np.frexp(amax)[1] - 1 + 127, 0) - down, 1)
    scale = np.exp2(byte - 127.0)
    codes = (blocks / scale).astype(np.float32).astype(dtype).astype(np.float64)
    return np.moveaxis((codes * scale).reshape(v.shape), -1, axis)


WIDE = False


def mx_kscale(k):
    if not WIDE:
        return np.ones(k)
    levels = np.array([10, -10, 5, -5, 0])
    a = np.random.permutation(np.resize(levels, k // 512 * 4)).reshape(k // 512, 4)
    idx = np.arange(k)
    return np.exp2(a[idx // 512, idx % 128 // 32])


BF16 = ml_dtypes.bfloat16


def bf(x):
    return np.asarray(x, np.float32).astype(BF16)


def f64(x):
    return np.asarray(x).astype(np.float64)


N, D_IN, D_H, D_OUT = 2048, 256, 512, 256
THRESH = 1e-6
EPS = 1e-8
DEG, BG, DEAD, TINY = 16.0, 4.0, 0.125, 1e-15


def draw_mobility():
    u = np.random.random_sample((N, N))
    strong = np.random.random_sample((N, N)) < DEG / N
    dead = np.random.random_sample(N) < DEAD
    return u * (BG / N + strong) * np.where(dead, TINY, 1.0)[None, :]


def setup_inputs():
    s = mx_kscale(D_H)
    return {'h1': bf(np.maximum(np.random.standard_normal((N, D_H)), 0.0) * s),
            'mobility_matrix': bf(draw_mobility()),
            'W_in': bf(np.random.standard_normal((D_H, D_OUT)) * 2.0 / np.sqrt(D_H) / s[:, None]),
            'b_in': bf(np.random.standard_normal(D_OUT) * 0.2)}


def reference(h1, mobility_matrix, W_in, b_in):
    h = f64(h1)
    M = f64(mobility_matrix)
    A = M / (M.sum(axis=0, keepdims=True) + EPS)
    mask = A > THRESH
    W = np.where(mask, A, 0.0)
    T = (mxq(h, 1, 'e4m3') @ mxq(f64(W_in), 0, 'e4m3')) + f64(b_in)
    weighted_sum = mxq(W, 0, 'e4m3').T @ mxq(T, 0, 'e4m3')
    weight_sum = W.sum(axis=0)
    has_edge = mask.any(axis=0)
    return np.where(has_edge[:, None], weighted_sum / (weight_sum[:, None] + EPS), T)

@@ -1,0 +1,296 @@
+from contextlib import ExitStack
+
+import concourse.mybir as mybir
+from concourse.masks import make_identity
+
+F32 = mybir.dt.float32
+BF16 = mybir.dt.bfloat16
+U32 = mybir.dt.uint32
+U8 = mybir.dt.uint8
+FP8X4 = mybir.dt.float8_e4m3fn_x4
+ALU = mybir.AluOpType
+ACT = mybir.ActivationFunctionType
+AXIS_X = mybir.AxisListType.X
+
+P = 128
+PACK = 4
+K_PASS = P * PACK
+
+N_NODES = 2048
+D_H = 512
+D_OUT = 256
+THRESH = 1e-6
+EPS = 1e-8
+
+GROUPS = N_NODES // K_PASS
+BLOCK = 512
+BLOCKS = N_NODES // BLOCK
+TILES = BLOCK // P
+
+FLOPS = 2 * N_NODES * D_H * D_OUT + 2 * N_NODES * N_NODES * D_OUT
+
+
+def tile_mobilitygnn_pb_kernel(tc, h1, mobility_matrix, W_in, b_in, out):
+    nc = tc.nc
+    with ExitStack() as ctx:
+        keep = ctx.enter_context(tc.tile_pool(name="keep", bufs=1))
+        stage = ctx.enter_context(tc.tile_pool(name="stage", bufs=2))
+        small = ctx.enter_context(tc.tile_pool(name="small", bufs=2))
+        psum_one = ctx.enter_context(tc.psum_pool(name="psum_one", bufs=1))
+        psum_two = ctx.enter_context(tc.psum_pool(name="psum_two", bufs=2))
+
+        w_raw = keep.tile([P, PACK, D_OUT], BF16)
+        for u in range(2):
+            nc.sync.dma_start(
+                out=w_raw[:, 2 * u : 2 * u + 2, :],
+                in_=W_in[256 * u : 256 * (u + 1), :].rearrange("(q e) n -> q e n", e=2),
+            )
+        bias_all = keep.tile([P, D_OUT], BF16)
+        nc.scalar.dma_start(out=bias_all[:], in_=b_in.partition_broadcast(P))
+        h1_sb = []
+        for g in range(GROUPS):
+            h1_rows = keep.tile([P, PACK, D_H], BF16, name="h1_rows_%d" % g)
+            nc.sync.dma_start(
+                out=h1_rows[:],
+                in_=h1[K_PASS * g : K_PASS * (g + 1), :].rearrange("(t p) k -> p t k", p=P),
+            )
+            h1_sb.append(h1_rows)
+        m_sb = {}
+        for b in range(BLOCKS):
+            for g in range(GROUPS):
+                m_chunk = keep.tile([P, PACK, BLOCK], BF16, name="m_%d_%d" % (b, g))
+                nc.sync.dma_start(
+                    out=m_chunk[:],
+                    in_=mobility_matrix[
+                        K_PASS * g : K_PASS * (g + 1), BLOCK * b : BLOCK * (b + 1)
+                    ].rearrange("(t p) i -> p t i", p=P),
+                )
+                m_sb[(b, g)] = m_chunk
+
+        ident_f32 = keep.tile([P, P], F32)
+        make_identity(nc, ident_f32[:])
+        ident_bf = keep.tile([P, P], BF16)
+        make_identity(nc, ident_bf[:])
+        ones_bf = keep.tile([P, 1], BF16)
+        nc.vector.memset(ones_bf[:], 1.0)
+
+        w_grouped = keep.tile([P, D_OUT, PACK], BF16, align_bytes=64)
+        nc.vector.tensor_copy(out=w_grouped[:], in_=w_raw[:].rearrange("q t n -> q n t"))
+        w_codes = keep.tile([P, D_OUT], U32, align_bytes=64)
+        w_scales = keep.tile([P, D_OUT], U8, align_bytes=64)
+        nc.vector.quantize_mx(
+            out=w_codes[:].bitcast(FP8X4),
+            scales=w_scales[:],
+            in_=w_grouped[:].rearrange("q n t -> q (n t)"),
+        )
+
+        h_codes = keep.tile([P, N_NODES], U32, align_bytes=64)
+        h_scales = keep.tile([P, N_NODES], U8, align_bytes=64)
+        t_f32 = keep.tile([P, GROUPS * PACK, D_OUT], F32)
+        t_grouped = keep.tile([P, GROUPS, D_OUT * PACK], BF16, align_bytes=64)
+        t_codes = keep.tile([P, GROUPS, D_OUT], U32, align_bytes=64)
+        t_scales = keep.tile([P, GROUPS, D_OUT], U8, align_bytes=64)
+        for g in range(GROUPS):
+            rows = slice(K_PASS * g, K_PASS * (g + 1))
+            h_grouped = stage.tile([P, K_PASS * PACK], BF16, align_bytes=64)
+            h_words = h_grouped[:].bitcast(F32).rearrange("q (t j u) -> q t j u", t=PACK, u=2)
+            for half in range(2):
+                turned = psum_two.tile([P, 2, 2, P], F32, tag="front")
+                for t2 in range(2):
+                    for u in range(2):
+                        nc.tensor.transpose(
+                            turned[:, t2, u, :],
+                            h1_sb[g][:, 2 * half + t2, :].bitcast(F32)[:, P * u : P * (u + 1)],
+                            ident_f32[:],
+                        )
+                nc.scalar.copy(
+                    out=h_words[:, 2 * half : 2 * half + 2, :, :],
+                    in_=turned[:].rearrange("q t u j -> q t j u"),
+                )
+            nc.vector.quantize_mx(
+                out=h_codes[:, rows].bitcast(FP8X4), scales=h_scales[:, rows], in_=h_grouped[:]
+            )
+            for half in range(2):
+                t_ps = psum_two.tile([P, 2, D_OUT], F32, tag="front")
+                first = PACK * g + 2 * half
+                for t2 in range(2):
+                    cols = slice(P * (first + t2), P * (first + t2 + 1))
+                    nc.tensor.matmul_mx(
+                        out=t_ps[:, t2, :],
+                        lhsT=h_codes[:, cols].bitcast(FP8X4),
+                        lhsT_scale=h_scales[:, cols],
+                        rhs=w_codes[:].bitcast(FP8X4),
+                        rhs_scale=w_scales[:],
+                        start=True,
+                        stop=True,
+                    )
+                nc.vector.tensor_tensor(
+                    out=t_f32[:, first : first + 2, :],
+                    in0=t_ps[:],
+                    in1=bias_all[:].unsqueeze(1).to_broadcast([P, 2, D_OUT]),
+                    op=ALU.add,
+                )
+            nc.scalar.copy(
+                out=t_grouped[:, g, :].rearrange("p (d t) -> p d t", t=PACK),
+                in_=t_f32[:, PACK * g : PACK * (g + 1), :].rearrange("p t d -> p d t"),
+            )
+        for g in range(GROUPS):
+            nc.vector.quantize_mx(
+                out=t_codes[:, g, :].bitcast(FP8X4), scales=t_scales[:, g, :], in_=t_grouped[:, g, :]
+            )
+
+        recip = keep.tile([P, BLOCKS * TILES], F32)
+        a_codes = keep.tile([P, GROUPS, N_NODES], U32, align_bytes=64)
+        a_scales = keep.tile([P, GROUPS, N_NODES], U8, align_bytes=64)
+        recip_all = {}
+        thresh_all = {}
+        kept_sums = {}
+        grouped = {}
+
+        def column_statistics(b):
+            sums_ps = psum_one.tile([P, TILES, GROUPS], F32, tag="sums")
+            for g in range(GROUPS):
+                for a in range(TILES):
+                    for t in range(PACK):
+                        nc.tensor.matmul(
+                            out=sums_ps[:, a, g : g + 1],
+                            lhsT=m_sb[(b, g)][:, t, P * a : P * (a + 1)],
+                            rhs=ones_bf[:],
+                            start=(t == 0),
+                            stop=(t == PACK - 1),
+                        )
+            tiles = slice(TILES * b, TILES * (b + 1))
+            denom = small.tile([P, TILES], F32)
+            nc.vector.tensor_reduce(out=denom[:], in_=sums_ps[:], axis=AXIS_X, op=ALU.add)
+            nc.vector.tensor_scalar_add(out=denom[:], in0=denom[:], scalar1=EPS)
+            nc.vector.reciprocal(out=recip[:, tiles], in_=denom[:])
+            thresh_f32 = small.tile([P, TILES], F32)
+            nc.vector.tensor_scalar_mul(out=thresh_f32[:], in0=denom[:], scalar1=THRESH)
+            thresh_bf = small.tile([P, TILES], BF16)
+            nc.vector.tensor_copy(
+                out=thresh_bf[:],
+                in_=thresh_f32[:].bitcast(BF16).rearrange("p (a h) -> p a h", h=2)[:, :, 1],
+            )
+            recip_ps = psum_two.tile([P, BLOCK], F32, tag="spread")
+            thresh_ps = psum_two.tile([P, BLOCK], F32, tag="spread")
+            for a in range(TILES):
+                cols = slice(P * a, P * (a + 1))
+                nc.tensor.matmul(
+                    out=recip_ps[:, cols],
+                    lhsT=recip[:, TILES * b + a : TILES * b + a + 1].to_broadcast([P, P]),
+                    rhs=ident_f32[:],
+                    start=True,
+                    stop=True,
+                )
+                nc.tensor.matmul(
+                    out=thresh_ps[:, cols],
+                    lhsT=thresh_bf[:, a : a + 1].to_broadcast([P, P]),
+                    rhs=ident_bf[:],
+                    start=True,
+                    stop=True,
+                )
+            recip_all[b] = keep.tile([P, BLOCK], F32, name="recip_all_%d" % b)
+            nc.scalar.copy(out=recip_all[b][:], in_=recip_ps[:])
+            thresh_all[b] = keep.tile([P, BLOCK], BF16, name="thresh_all_%d" % b)
+            nc.scalar.copy(out=thresh_all[b][:], in_=thresh_ps[:])
+
+        def weigh(b, g):
+            if g == 0:
+                kept_sums[b] = psum_one.tile([P, TILES, GROUPS], F32, tag="kept_sums", name="kept_sums_ps")
+            m_chunk = m_sb[(b, g)]
+            kept = stage.tile([P, PACK, BLOCK], BF16)
+            nc.vector.tensor_tensor(
+                out=kept[:],
+                in0=m_chunk[:],
+                in1=thresh_all[b][:].unsqueeze(1).to_broadcast([P, PACK, BLOCK]),
+                op=ALU.is_gt,
+            )
+            nc.vector.tensor_tensor(out=kept[:], in0=kept[:], in1=m_chunk[:], op=ALU.mult)
+            for a in range(TILES):
+                for t in range(PACK):
+                    nc.tensor.matmul(
+                        out=kept_sums[b][:, a, g : g + 1],
+                        lhsT=kept[:, t, P * a : P * (a + 1)],
+                        rhs=ones_bf[:],
+                        start=(t == 0),
+                        stop=(t == PACK - 1),
+                    )
+            grouped[(b, g)] = stage.tile([P, BLOCK, PACK], BF16, align_bytes=64, name="grouped")
+            nc.vector.tensor_tensor(
+                out=grouped[(b, g)][:],
+                in0=kept[:].rearrange("p t i -> p i t"),
+                in1=recip_all[b][:].unsqueeze(2).to_broadcast([P, BLOCK, PACK]),
+                op=ALU.mult,
+            )
+
+        def quantise(b, g):
+            cols = slice(BLOCK * b, BLOCK * (b + 1))
+            nc.vector.quantize_mx(
+                out=a_codes[:, g, cols].bitcast(FP8X4),
+                scales=a_scales[:, g, cols],
+                in_=grouped[(b, g)][:].rearrange("p i t -> p (i t)"),
+            )
+
+        def aggregate(b):
+            tiles = slice(TILES * b, TILES * (b + 1))
+            kept_sum = small.tile([P, TILES], F32)
+            nc.vector.tensor_reduce(out=kept_sum[:], in_=kept_sums[b][:], axis=AXIS_X, op=ALU.add)
+            has_edge = small.tile([P, TILES], F32)
+            nc.vector.tensor_single_scalar(out=has_edge[:], in_=kept_sum[:], scalar=0.0, op=ALU.is_gt)
+            no_edge = small.tile([P, TILES], F32)
+            nc.vector.tensor_scalar(
+                out=no_edge[:], in0=has_edge[:], scalar1=-1.0, scalar2=1.0, op0=ALU.mult, op1=ALU.add
+            )
+            wsum = small.tile([P, TILES], F32)
+            nc.vector.tensor_tensor(out=wsum[:], in0=kept_sum[:], in1=recip[:, tiles], op=ALU.mult)
+            nc.vector.tensor_scalar_add(out=wsum[:], in0=wsum[:], scalar1=EPS)
+            share = small.tile([P, TILES], F32)
+            nc.vector.reciprocal(out=share[:], in_=wsum[:])
+            nc.vector.tensor_tensor(out=share[:], in0=share[:], in1=has_edge[:], op=ALU.mult)
+            for half in range(TILES // 2):
+                ws_ps = psum_two.tile([P, 2, D_OUT], F32, tag="ws")
+                fallback = stage.tile([P, 2, D_OUT], F32)
+                result = stage.tile([P, 2, D_OUT], F32)
+                for a2 in range(2):
+                    a = 2 * half + a2
+                    c = TILES * b + a
+                    cols = slice(P * c, P * (c + 1))
+                    for g in range(GROUPS):
+                        nc.tensor.matmul_mx(
+                            out=ws_ps[:, a2, :],
+                            lhsT=a_codes[:, g, cols].bitcast(FP8X4),
+                            lhsT_scale=a_scales[:, g, cols],
+                            rhs=t_codes[:, g, :].bitcast(FP8X4),
+                            rhs_scale=t_scales[:, g, :],
+                            start=(g == 0),
+                            stop=(g == GROUPS - 1),
+                        )
+                    nc.scalar.activation(
+                        out=fallback[:, a2, :], in_=t_f32[:, c, :], func=ACT.Copy, scale=no_edge[:, a : a + 1]
+                    )
+                    nc.vector.scalar_tensor_tensor(
+                        out=result[:, a2, :],
+                        in0=ws_ps[:, a2, :],
+                        scalar=share[:, a : a + 1],
+                        in1=fallback[:, a2, :],
+                        op0=ALU.mult,
+                        op1=ALU.add,
+                    )
+                first_row = P * (TILES * b + 2 * half)
+                nc.sync.dma_start(
+                    out=out[first_row : first_row + 2 * P, :].rearrange("(a p) d -> p a d", p=P),
+                    in_=result[:],
+                )
+
+        chunks = [(b, g) for b in range(BLOCKS) for g in range(GROUPS)]
+        column_statistics(0)
+        for n, (b, g) in enumerate(chunks):
+            if g == 0 and b + 1 < BLOCKS:
+                column_statistics(b + 1)
+            weigh(b, g)
+            if n > 0:
+                quantise(*chunks[n - 1])
+                if g == 0:
+                    aggregate(b - 1)
+        quantise(*chunks[-1])
+        aggregate(BLOCKS - 1)

@@ -26,6 +26,9 @@ GROUPS = N_NODES // K_PASS
 BLOCK = 512
 BLOCKS = N_NODES // BLOCK
 TILES = BLOCK // P
+HALVES = 2
+UNIT_GROUPS = GROUPS // HALVES
+UNIT_ROWS = UNIT_GROUPS * K_PASS
 
 FLOPS = 2 * N_NODES * D_H * D_OUT + 2 * N_NODES * N_NODES * D_OUT
 
@@ -34,10 +37,9 @@ def tile_mobilitygnn_pb_kernel(tc, h1, mobility_matrix, W_in, b_in, out):
     nc = tc.nc
     with ExitStack() as ctx:
         keep = ctx.enter_context(tc.tile_pool(name="keep", bufs=1))
-        stage = ctx.enter_context(tc.tile_pool(name="stage", bufs=2))
+        stage = ctx.enter_context(tc.tile_pool(name="stage", bufs=3))
         small = ctx.enter_context(tc.tile_pool(name="small", bufs=2))
-        psum_one = ctx.enter_context(tc.psum_pool(name="psum_one", bufs=1))
-        psum_two = ctx.enter_context(tc.psum_pool(name="psum_two", bufs=2))
+        psum = ctx.enter_context(tc.psum_pool(name="psum", bufs=2))
 
         w_raw = keep.tile([P, PACK, D_OUT], BF16)
         for u in range(2):
@@ -95,23 +97,23 @@ def tile_mobilitygnn_pb_kernel(tc, h1, mobility_matrix, W_in, b_in, out):
             h_grouped = stage.tile([P, K_PASS * PACK], BF16, align_bytes=64)
             h_words = h_grouped[:].bitcast(F32).rearrange("q (t j u) -> q t j u", t=PACK, u=2)
             for half in range(2):
-                turned = psum_two.tile([P, 2, 2, P], F32, tag="front")
+                h_turned = psum.tile([P, 2, 2, P], F32, tag="turned")
                 for t2 in range(2):
                     for u in range(2):
                         nc.tensor.transpose(
-                            turned[:, t2, u, :],
+                            h_turned[:, t2, u, :],
                             h1_sb[g][:, 2 * half + t2, :].bitcast(F32)[:, P * u : P * (u + 1)],
                             ident_f32[:],
                         )
                 nc.scalar.copy(
                     out=h_words[:, 2 * half : 2 * half + 2, :, :],
-                    in_=turned[:].rearrange("q t u j -> q t j u"),
+                    in_=h_turned[:].rearrange("q t u j -> q t j u"),
                 )
             nc.vector.quantize_mx(
                 out=h_codes[:, rows].bitcast(FP8X4), scales=h_scales[:, rows], in_=h_grouped[:]
             )
             for half in range(2):
-                t_ps = psum_two.tile([P, 2, D_OUT], F32, tag="front")
+                t_ps = psum.tile([P, 2, D_OUT], F32, tag="back")
                 first = PACK * g + 2 * half
                 for t2 in range(2):
                     cols = slice(P * (first + t2), P * (first + t2 + 1))
@@ -140,157 +142,179 @@ def tile_mobilitygnn_pb_kernel(tc, h1, mobility_matrix, W_in, b_in, out):
             )
 
         recip = keep.tile([P, BLOCKS * TILES], F32)
-        a_codes = keep.tile([P, GROUPS, N_NODES], U32, align_bytes=64)
-        a_scales = keep.tile([P, GROUPS, N_NODES], U8, align_bytes=64)
-        recip_all = {}
-        thresh_all = {}
-        kept_sums = {}
-        grouped = {}
+        thresh = keep.tile([P, BLOCKS * TILES], F32)
+        wsum_parts = keep.tile([P, BLOCKS * TILES, HALVES], F32)
+        a_codes = keep.tile([P, BLOCKS * TILES, GROUPS * P], U32, align_bytes=64)
+        a_scales = keep.tile([P, BLOCKS * TILES, GROUPS * P], U8, align_bytes=64)
 
-        def column_statistics(b):
-            sums_ps = psum_one.tile([P, TILES, GROUPS], F32, tag="sums")
-            for g in range(GROUPS):
-                for a in range(TILES):
+        units = [(b, a, h) for b in range(BLOCKS) for a in range(TILES) for h in range(HALVES)]
+        sums_ps = {}
+        turned = {}
+        kept = {}
+        weights = {}
+        back = {}
+        grouped = {}
+        ws_ps = {}
+
+        def column_sums(b):
+            sums_ps[b] = psum.tile([P, TILES], F32, tag="sums", name="sums_ps")
+            for a in range(TILES):
+                for g in range(GROUPS):
                     for t in range(PACK):
                         nc.tensor.matmul(
-                            out=sums_ps[:, a, g : g + 1],
+                            out=sums_ps[b][:, a : a + 1],
                             lhsT=m_sb[(b, g)][:, t, P * a : P * (a + 1)],
                             rhs=ones_bf[:],
-                            start=(t == 0),
-                            stop=(t == PACK - 1),
+                            start=(g == 0 and t == 0),
+                            stop=(g == GROUPS - 1 and t == PACK - 1),
                         )
+
+        def column_scalars(b):
             tiles = slice(TILES * b, TILES * (b + 1))
             denom = small.tile([P, TILES], F32)
-            nc.vector.tensor_reduce(out=denom[:], in_=sums_ps[:], axis=AXIS_X, op=ALU.add)
-            nc.vector.tensor_scalar_add(out=denom[:], in0=denom[:], scalar1=EPS)
-            nc.vector.reciprocal(out=recip[:, tiles], in_=denom[:])
-            thresh_f32 = small.tile([P, TILES], F32)
-            nc.vector.tensor_scalar_mul(out=thresh_f32[:], in0=denom[:], scalar1=THRESH)
-            thresh_bf = small.tile([P, TILES], BF16)
-            nc.vector.tensor_copy(
-                out=thresh_bf[:],
-                in_=thresh_f32[:].bitcast(BF16).rearrange("p (a h) -> p a h", h=2)[:, :, 1],
-            )
-            recip_ps = psum_two.tile([P, BLOCK], F32, tag="spread")
-            thresh_ps = psum_two.tile([P, BLOCK], F32, tag="spread")
-            for a in range(TILES):
-                cols = slice(P * a, P * (a + 1))
-                nc.tensor.matmul(
-                    out=recip_ps[:, cols],
-                    lhsT=recip[:, TILES * b + a : TILES * b + a + 1].to_broadcast([P, P]),
-                    rhs=ident_f32[:],
-                    start=True,
-                    stop=True,
-                )
-                nc.tensor.matmul(
-                    out=thresh_ps[:, cols],
-                    lhsT=thresh_bf[:, a : a + 1].to_broadcast([P, P]),
-                    rhs=ident_bf[:],
-                    start=True,
-                    stop=True,
-                )
-            recip_all[b] = keep.tile([P, BLOCK], F32, name="recip_all_%d" % b)
-            nc.scalar.copy(out=recip_all[b][:], in_=recip_ps[:])
-            thresh_all[b] = keep.tile([P, BLOCK], BF16, name="thresh_all_%d" % b)
-            nc.scalar.copy(out=thresh_all[b][:], in_=thresh_ps[:])
-
-        def weigh(b, g):
-            if g == 0:
-                kept_sums[b] = psum_one.tile([P, TILES, GROUPS], F32, tag="kept_sums", name="kept_sums_ps")
-            m_chunk = m_sb[(b, g)]
-            kept = stage.tile([P, PACK, BLOCK], BF16)
-            nc.vector.tensor_tensor(
-                out=kept[:],
-                in0=m_chunk[:],
-                in1=thresh_all[b][:].unsqueeze(1).to_broadcast([P, PACK, BLOCK]),
-                op=ALU.is_gt,
-            )
-            nc.vector.tensor_tensor(out=kept[:], in0=kept[:], in1=m_chunk[:], op=ALU.mult)
-            for a in range(TILES):
-                for t in range(PACK):
-                    nc.tensor.matmul(
-                        out=kept_sums[b][:, a, g : g + 1],
-                        lhsT=kept[:, t, P * a : P * (a + 1)],
-                        rhs=ones_bf[:],
-                        start=(t == 0),
-                        stop=(t == PACK - 1),
-                    )
-            grouped[(b, g)] = stage.tile([P, BLOCK, PACK], BF16, align_bytes=64, name="grouped")
-            nc.vector.tensor_tensor(
-                out=grouped[(b, g)][:],
-                in0=kept[:].rearrange("p t i -> p i t"),
-                in1=recip_all[b][:].unsqueeze(2).to_broadcast([P, BLOCK, PACK]),
-                op=ALU.mult,
-            )
-
-        def quantise(b, g):
-            cols = slice(BLOCK * b, BLOCK * (b + 1))
-            nc.vector.quantize_mx(
-                out=a_codes[:, g, cols].bitcast(FP8X4),
-                scales=a_scales[:, g, cols],
-                in_=grouped[(b, g)][:].rearrange("p i t -> p (i t)"),
-            )
-
-        def aggregate(b):
-            tiles = slice(TILES * b, TILES * (b + 1))
-            kept_sum = small.tile([P, TILES], F32)
-            nc.vector.tensor_reduce(out=kept_sum[:], in_=kept_sums[b][:], axis=AXIS_X, op=ALU.add)
-            has_edge = small.tile([P, TILES], F32)
-            nc.vector.tensor_single_scalar(out=has_edge[:], in_=kept_sum[:], scalar=0.0, op=ALU.is_gt)
-            no_edge = small.tile([P, TILES], F32)
+            nc.vector.tensor_scalar_add(out=denom[:], in0=sums_ps[b][:], scalar1=EPS)
             nc.vector.tensor_scalar(
-                out=no_edge[:], in0=has_edge[:], scalar1=-1.0, scalar2=1.0, op0=ALU.mult, op1=ALU.add
+                out=thresh[:, tiles], in0=sums_ps[b][:], scalar1=EPS, scalar2=THRESH, op0=ALU.add, op1=ALU.mult
             )
+            nc.vector.reciprocal(out=recip[:, tiles], in_=denom[:])
+
+        def turn(n):
+            b, a, h = units[n]
+            turned[n] = psum.tile([P, UNIT_GROUPS * PACK, P], BF16, tag="turned", name="turned")
+            for g2 in range(UNIT_GROUPS):
+                for t in range(PACK):
+                    nc.tensor.transpose(
+                        turned[n][:, PACK * g2 + t, :],
+                        m_sb[(b, UNIT_GROUPS * h + g2)][:, t, P * a : P * (a + 1)],
+                        ident_bf[:],
+                    )
+
+        def drop_small(n):
+            b, a, h = units[n]
+            c = TILES * b + a
+            m_turned = turned[n][:].rearrange("p c j -> p (c j)")
+            kept[n] = stage.tile([P, UNIT_ROWS], BF16, name="kept")
+            nc.vector.tensor_scalar(
+                out=kept[n][:], in0=m_turned, scalar1=thresh[:, c : c + 1], scalar2=None, op0=ALU.is_gt
+            )
+            nc.vector.tensor_tensor(out=kept[n][:], in0=kept[n][:], in1=m_turned, op=ALU.mult)
+
+        def scale(n):
+            b, a, h = units[n]
+            c = TILES * b + a
+            weights[n] = stage.tile([P, UNIT_ROWS], BF16, name="weights")
+            nc.scalar.activation(
+                out=weights[n][:],
+                in_=kept[n][:],
+                func=ACT.Copy,
+                scale=recip[:, c : c + 1],
+                accum_out=wsum_parts[:, c, h : h + 1],
+            )
+
+        def turn_back(n):
+            back[n] = psum.tile([P, UNIT_GROUPS, PACK, P], BF16, tag="back", name="back")
+            for g2 in range(UNIT_GROUPS):
+                for t in range(PACK):
+                    row_tile = PACK * g2 + t
+                    nc.tensor.transpose(
+                        back[n][:, g2, t, :], weights[n][:, P * row_tile : P * (row_tile + 1)], ident_bf[:]
+                    )
+
+        def regroup(n):
+            grouped[n] = stage.tile([P, UNIT_GROUPS, P, PACK], BF16, align_bytes=64, name="grouped")
+            source = back[n][:].rearrange("p g t i -> p g i t")
+            if n % 3 == 2:
+                nc.vector.tensor_copy(out=grouped[n][:], in_=source)
+            else:
+                nc.scalar.copy(out=grouped[n][:], in_=source)
+
+        def quantise(n):
+            b, a, h = units[n]
+            c = TILES * b + a
+            cols = slice(UNIT_GROUPS * P * h, UNIT_GROUPS * P * (h + 1))
+            nc.vector.quantize_mx(
+                out=a_codes[:, c, cols].bitcast(FP8X4),
+                scales=a_scales[:, c, cols],
+                in_=grouped[n][:].rearrange("p g i t -> p (g i t)"),
+            )
+
+        def multiply(n):
+            b, a, h = units[n]
+            if h < HALVES - 1:
+                return
+            c = TILES * b + a
+            if a % 2 == 0:
+                ws_ps[c // 2] = psum.tile([P, 2, D_OUT], F32, tag="ws", name="ws_ps")
+            for g in range(GROUPS):
+                cols = slice(P * g, P * (g + 1))
+                nc.tensor.matmul_mx(
+                    out=ws_ps[c // 2][:, a % 2, :],
+                    lhsT=a_codes[:, c, cols].bitcast(FP8X4),
+                    lhsT_scale=a_scales[:, c, cols],
+                    rhs=t_codes[:, g, :].bitcast(FP8X4),
+                    rhs_scale=t_scales[:, g, :],
+                    start=(g == 0),
+                    stop=(g == GROUPS - 1),
+                )
+
+        def finish(b):
+            tiles = slice(TILES * b, TILES * (b + 1))
             wsum = small.tile([P, TILES], F32)
-            nc.vector.tensor_tensor(out=wsum[:], in0=kept_sum[:], in1=recip[:, tiles], op=ALU.mult)
-            nc.vector.tensor_scalar_add(out=wsum[:], in0=wsum[:], scalar1=EPS)
+            nc.vector.tensor_tensor(
+                out=wsum[:], in0=wsum_parts[:, tiles, 0], in1=wsum_parts[:, tiles, 1], op=ALU.add
+            )
+            no_edge = small.tile([P, TILES], F32)
+            nc.vector.tensor_single_scalar(out=no_edge[:], in_=wsum[:], scalar=0.0, op=ALU.is_le)
             share = small.tile([P, TILES], F32)
-            nc.vector.reciprocal(out=share[:], in_=wsum[:])
-            nc.vector.tensor_tensor(out=share[:], in0=share[:], in1=has_edge[:], op=ALU.mult)
-            for half in range(TILES // 2):
-                ws_ps = psum_two.tile([P, 2, D_OUT], F32, tag="ws")
+            nc.vector.tensor_scalar_add(out=share[:], in0=wsum[:], scalar1=EPS)
+            nc.vector.reciprocal(out=share[:], in_=share[:])
+            for pair in range(TILES // 2):
                 fallback = stage.tile([P, 2, D_OUT], F32)
                 result = stage.tile([P, 2, D_OUT], F32)
                 for a2 in range(2):
-                    a = 2 * half + a2
+                    a = 2 * pair + a2
                     c = TILES * b + a
-                    cols = slice(P * c, P * (c + 1))
-                    for g in range(GROUPS):
-                        nc.tensor.matmul_mx(
-                            out=ws_ps[:, a2, :],
-                            lhsT=a_codes[:, g, cols].bitcast(FP8X4),
-                            lhsT_scale=a_scales[:, g, cols],
-                            rhs=t_codes[:, g, :].bitcast(FP8X4),
-                            rhs_scale=t_scales[:, g, :],
-                            start=(g == 0),
-                            stop=(g == GROUPS - 1),
-                        )
                     nc.scalar.activation(
                         out=fallback[:, a2, :], in_=t_f32[:, c, :], func=ACT.Copy, scale=no_edge[:, a : a + 1]
                     )
                     nc.vector.scalar_tensor_tensor(
                         out=result[:, a2, :],
-                        in0=ws_ps[:, a2, :],
+                        in0=ws_ps[c // 2][:, a2, :],
                         scalar=share[:, a : a + 1],
                         in1=fallback[:, a2, :],
                         op0=ALU.mult,
                         op1=ALU.add,
                     )
-                first_row = P * (TILES * b + 2 * half)
+                first_row = P * (TILES * b + 2 * pair)
                 nc.sync.dma_start(
                     out=out[first_row : first_row + 2 * P, :].rearrange("(a p) d -> p a d", p=P),
                     in_=result[:],
                 )
 
-        chunks = [(b, g) for b in range(BLOCKS) for g in range(GROUPS)]
-        column_statistics(0)
-        for n, (b, g) in enumerate(chunks):
-            if g == 0 and b + 1 < BLOCKS:
-                column_statistics(b + 1)
-            weigh(b, g)
-            if n > 0:
-                quantise(*chunks[n - 1])
-                if g == 0:
-                    aggregate(b - 1)
-        quantise(*chunks[-1])
-        aggregate(BLOCKS - 1)
+        def live(n):
+            return 0 <= n < len(units)
+
+        per_block = TILES * HALVES
+        column_sums(0)
+        column_scalars(0)
+        for step in range(len(units) + 7):
+            if live(step):
+                turn(step)
+            if live(step - 1):
+                drop_small(step - 1)
+            if live(step - 2):
+                scale(step - 2)
+            if live(step - 3):
+                turn_back(step - 3)
+            if live(step - 4):
+                regroup(step - 4)
+            if live(step - 5):
+                quantise(step - 5)
+            if live(step - 6):
+                multiply(step - 6)
+            if live(step - 7) and (step - 7) % per_block == per_block - 1:
+                finish((step - 7) // per_block)
+            if step % per_block == 2 and step // per_block + 1 < BLOCKS:
+                column_sums(step // per_block + 1)
+            if step % per_block == 4 and step // per_block + 1 < BLOCKS:
+                column_scalars(step // per_block + 1)

@@ -40,6 +40,7 @@ def tile_mobilitygnn_pb_kernel(tc, h1, mobility_matrix, W_in, b_in, out):
         stage = ctx.enter_context(tc.tile_pool(name="stage", bufs=3))
         small = ctx.enter_context(tc.tile_pool(name="small", bufs=2))
         psum = ctx.enter_context(tc.psum_pool(name="psum", bufs=2))
+        ctx.enter_context(tc.manual_schedule())
 
         w_raw = keep.tile([P, PACK, D_OUT], BF16)
         for u in range(2):
@@ -112,6 +113,7 @@ def tile_mobilitygnn_pb_kernel(tc, h1, mobility_matrix, W_in, b_in, out):
             nc.vector.quantize_mx(
                 out=h_codes[:, rows].bitcast(FP8X4), scales=h_scales[:, rows], in_=h_grouped[:]
             )
+        for g in range(GROUPS):
             for half in range(2):
                 t_ps = psum.tile([P, 2, D_OUT], F32, tag="back")
                 first = PACK * g + 2 * half
@@ -136,10 +138,6 @@ def tile_mobilitygnn_pb_kernel(tc, h1, mobility_matrix, W_in, b_in, out):
                 out=t_grouped[:, g, :].rearrange("p (d t) -> p d t", t=PACK),
                 in_=t_f32[:, PACK * g : PACK * (g + 1), :].rearrange("p t d -> p d t"),
             )
-        for g in range(GROUPS):
-            nc.vector.quantize_mx(
-                out=t_codes[:, g, :].bitcast(FP8X4), scales=t_scales[:, g, :], in_=t_grouped[:, g, :]
-            )
 
         recip = keep.tile([P, BLOCKS * TILES], F32)
         thresh = keep.tile([P, BLOCKS * TILES], F32)
@@ -156,18 +154,18 @@ def tile_mobilitygnn_pb_kernel(tc, h1, mobility_matrix, W_in, b_in, out):
         grouped = {}
         ws_ps = {}
 
-        def column_sums(b):
-            sums_ps[b] = psum.tile([P, TILES], F32, tag="sums", name="sums_ps")
-            for a in range(TILES):
-                for g in range(GROUPS):
-                    for t in range(PACK):
-                        nc.tensor.matmul(
-                            out=sums_ps[b][:, a : a + 1],
-                            lhsT=m_sb[(b, g)][:, t, P * a : P * (a + 1)],
-                            rhs=ones_bf[:],
-                            start=(g == 0 and t == 0),
-                            stop=(g == GROUPS - 1 and t == PACK - 1),
-                        )
+        def column_sums(b, a):
+            if a == 0:
+                sums_ps[b] = psum.tile([P, TILES], F32, tag="sums", name="sums_ps")
+            for g in range(GROUPS):
+                for t in range(PACK):
+                    nc.tensor.matmul(
+                        out=sums_ps[b][:, a : a + 1],
+                        lhsT=m_sb[(b, g)][:, t, P * a : P * (a + 1)],
+                        rhs=ones_bf[:],
+                        start=(g == 0 and t == 0),
+                        stop=(g == GROUPS - 1 and t == PACK - 1),
+                    )
 
         def column_scalars(b):
             tiles = slice(TILES * b, TILES * (b + 1))
@@ -240,12 +238,10 @@ def tile_mobilitygnn_pb_kernel(tc, h1, mobility_matrix, W_in, b_in, out):
 
         def multiply(n):
             b, a, h = units[n]
-            if h < HALVES - 1:
-                return
             c = TILES * b + a
-            if a % 2 == 0:
+            if h == 0 and a % 2 == 0:
                 ws_ps[c // 2] = psum.tile([P, 2, D_OUT], F32, tag="ws", name="ws_ps")
-            for g in range(GROUPS):
+            for g in range(UNIT_GROUPS * h, UNIT_GROUPS * (h + 1)):
                 cols = slice(P * g, P * (g + 1))
                 nc.tensor.matmul_mx(
                     out=ws_ps[c // 2][:, a % 2, :],
@@ -257,47 +253,72 @@ def tile_mobilitygnn_pb_kernel(tc, h1, mobility_matrix, W_in, b_in, out):
                     stop=(g == GROUPS - 1),
                 )
 
-        def finish(b):
+        share = {}
+        no_edge = {}
+        fallback = {}
+        result = {}
+
+        def shares(b):
             tiles = slice(TILES * b, TILES * (b + 1))
-            wsum = small.tile([P, TILES], F32)
-            nc.vector.tensor_tensor(
-                out=wsum[:], in0=wsum_parts[:, tiles, 0], in1=wsum_parts[:, tiles, 1], op=ALU.add
+            denom = small.tile([P, TILES], F32, name="wsum_eps")
+            nc.vector.scalar_tensor_tensor(
+                out=denom[:],
+                in0=wsum_parts[:, tiles, 0],
+                scalar=EPS,
+                in1=wsum_parts[:, tiles, 1],
+                op0=ALU.add,
+                op1=ALU.add,
             )
-            no_edge = small.tile([P, TILES], F32)
-            nc.vector.tensor_single_scalar(out=no_edge[:], in_=wsum[:], scalar=0.0, op=ALU.is_le)
-            share = small.tile([P, TILES], F32)
-            nc.vector.tensor_scalar_add(out=share[:], in0=wsum[:], scalar1=EPS)
-            nc.vector.reciprocal(out=share[:], in_=share[:])
-            for pair in range(TILES // 2):
-                fallback = stage.tile([P, 2, D_OUT], F32)
-                result = stage.tile([P, 2, D_OUT], F32)
-                for a2 in range(2):
-                    a = 2 * pair + a2
-                    c = TILES * b + a
-                    nc.scalar.activation(
-                        out=fallback[:, a2, :], in_=t_f32[:, c, :], func=ACT.Copy, scale=no_edge[:, a : a + 1]
-                    )
-                    nc.vector.scalar_tensor_tensor(
-                        out=result[:, a2, :],
-                        in0=ws_ps[c // 2][:, a2, :],
-                        scalar=share[:, a : a + 1],
-                        in1=fallback[:, a2, :],
-                        op0=ALU.mult,
-                        op1=ALU.add,
-                    )
-                first_row = P * (TILES * b + 2 * pair)
+            no_edge[b] = small.tile([P, TILES], F32, name="no_edge")
+            nc.vector.tensor_single_scalar(out=no_edge[b][:], in_=denom[:], scalar=EPS, op=ALU.is_le)
+            share[b] = small.tile([P, TILES], F32, name="share")
+            nc.vector.reciprocal(out=share[b][:], in_=denom[:])
+
+        def fall_back(b, a):
+            c = TILES * b + a
+            if a % 2 == 0:
+                fallback[c // 2] = stage.tile([P, 2, D_OUT], F32, name="fallback")
+            nc.scalar.activation(
+                out=fallback[c // 2][:, a % 2, :],
+                in_=t_f32[:, c, :],
+                func=ACT.Copy,
+                scale=no_edge[b][:, a : a + 1],
+            )
+
+        def finish(b, a):
+            c = TILES * b + a
+            if a % 2 == 0:
+                result[c // 2] = stage.tile([P, 2, D_OUT], F32, name="result")
+            nc.vector.scalar_tensor_tensor(
+                out=result[c // 2][:, a % 2, :],
+                in0=ws_ps[c // 2][:, a % 2, :],
+                scalar=share[b][:, a : a + 1],
+                in1=fallback[c // 2][:, a % 2, :],
+                op0=ALU.mult,
+                op1=ALU.add,
+            )
+            if a % 2 == 1:
+                first_row = P * (c - 1)
                 nc.sync.dma_start(
                     out=out[first_row : first_row + 2 * P, :].rearrange("(a p) d -> p a d", p=P),
-                    in_=result[:],
+                    in_=result[c // 2][:],
                 )
 
         def live(n):
             return 0 <= n < len(units)
 
         per_block = TILES * HALVES
-        column_sums(0)
+        for a in range(TILES):
+            column_sums(0, a)
         column_scalars(0)
-        for step in range(len(units) + 7):
+        nc.vector.quantize_mx(
+            out=t_codes[:].rearrange("p g d -> p (g d)").bitcast(FP8X4),
+            scales=t_scales[:].rearrange("p g d -> p (g d)"),
+            in_=t_grouped[:].rearrange("p g x -> p (g x)"),
+        )
+        for step in range(len(units) + per_block):
+            if step > 0 and step % per_block == 0 and step // per_block < BLOCKS:
+                column_scalars(step // per_block)
             if live(step):
                 turn(step)
             if live(step - 1):
@@ -312,9 +333,13 @@ def tile_mobilitygnn_pb_kernel(tc, h1, mobility_matrix, W_in, b_in, out):
                 quantise(step - 5)
             if live(step - 6):
                 multiply(step - 6)
-            if live(step - 7) and (step - 7) % per_block == per_block - 1:
-                finish((step - 7) // per_block)
-            if step % per_block == 2 and step // per_block + 1 < BLOCKS:
-                column_sums(step // per_block + 1)
-            if step % per_block == 4 and step // per_block + 1 < BLOCKS:
-                column_scalars(step // per_block + 1)
+            if step % per_block >= TILES and step // per_block + 1 < BLOCKS:
+                column_sums(step // per_block + 1, step % per_block - TILES)
+            b, late = divmod(step - per_block - 2, per_block)
+            if 0 <= b < BLOCKS:
+                if late == 0:
+                    shares(b)
+                if 1 <= late <= TILES:
+                    fall_back(b, late - 1)
+                if 2 <= late <= TILES + 1:
+                    finish(b, late - 2)

@@ -40,6 +40,7 @@ def tile_mobilitygnn_pb_kernel(tc, h1, mobility_matrix, W_in, b_in, out):
         stage = ctx.enter_context(tc.tile_pool(name="stage", bufs=3))
         small = ctx.enter_context(tc.tile_pool(name="small", bufs=2))
         psum = ctx.enter_context(tc.psum_pool(name="psum", bufs=2))
+        psum_one = ctx.enter_context(tc.psum_pool(name="psum_one", bufs=1))
         ctx.enter_context(tc.manual_schedule())
 
         w_raw = keep.tile([P, PACK, D_OUT], BF16)
@@ -156,7 +157,7 @@ def tile_mobilitygnn_pb_kernel(tc, h1, mobility_matrix, W_in, b_in, out):
 
         def column_sums(b, a):
             if a == 0:
-                sums_ps[b] = psum.tile([P, TILES], F32, tag="sums", name="sums_ps")
+                sums_ps[b] = psum_one.tile([P, TILES], F32, tag="sums", name="sums_ps")
             for g in range(GROUPS):
                 for t in range(PACK):
                     nc.tensor.matmul(
@@ -251,6 +252,18 @@ def tile_mobilitygnn_pb_kernel(tc, h1, mobility_matrix, W_in, b_in, out):
                     rhs_scale=t_scales[:, g, :],
                     start=(g == 0),
                     stop=(g == GROUPS - 1),
+                )
+            unread = psum_one.tile([P, D_OUT], F32, tag="unread")
+            for g in range(UNIT_GROUPS * h, UNIT_GROUPS * (h + 1)):
+                cols = slice(P * g, P * (g + 1))
+                nc.tensor.matmul_mx(
+                    out=unread[:],
+                    lhsT=a_codes[:, c, cols].bitcast(FP8X4),
+                    lhsT_scale=a_scales[:, c, cols],
+                    rhs=t_codes[:, g, :].bitcast(FP8X4),
+                    rhs_scale=t_scales[:, g, :],
+                    start=(g == UNIT_GROUPS * h),
+                    stop=(g == UNIT_GROUPS * (h + 1) - 1),
                 )
 
         share = {}

@@ -29,6 +29,7 @@ TILES = BLOCK // P
 HALVES = 2
 UNIT_GROUPS = GROUPS // HALVES
 UNIT_ROWS = UNIT_GROUPS * K_PASS
+RUN_OF_PASSES = 4
 
 FLOPS = 2 * N_NODES * D_H * D_OUT + 2 * N_NODES * N_NODES * D_OUT
 
@@ -63,12 +64,14 @@ def tile_mobilitygnn_pb_kernel(tc, h1, mobility_matrix, W_in, b_in, out):
         for b in range(BLOCKS):
             for g in range(GROUPS):
                 m_chunk = keep.tile([P, PACK, BLOCK], BF16, name="m_%d_%d" % (b, g))
-                nc.sync.dma_start(
-                    out=m_chunk[:],
-                    in_=mobility_matrix[
-                        K_PASS * g : K_PASS * (g + 1), BLOCK * b : BLOCK * (b + 1)
-                    ].rearrange("(t p) i -> p t i", p=P),
-                )
+                for e in range(2):
+                    first_row = K_PASS * g + 2 * P * e
+                    nc.sync.dma_start(
+                        out=m_chunk[e:P:2, :, :],
+                        in_=mobility_matrix[
+                            first_row : first_row + 2 * P, BLOCK * b : BLOCK * (b + 1)
+                        ].rearrange("(s q) i -> q s i", s=PACK),
+                    )
                 m_sb[(b, g)] = m_chunk
 
         ident_f32 = keep.tile([P, P], F32)
@@ -136,8 +139,8 @@ def tile_mobilitygnn_pb_kernel(tc, h1, mobility_matrix, W_in, b_in, out):
                     op=ALU.add,
                 )
             nc.scalar.copy(
-                out=t_grouped[:, g, :].rearrange("p (d t) -> p d t", t=PACK),
-                in_=t_f32[:, PACK * g : PACK * (g + 1), :].rearrange("p t d -> p d t"),
+                out=t_grouped[:, g, :].rearrange("p (d u e) -> p d u e", u=2, e=2),
+                in_=t_f32[:, PACK * g : PACK * (g + 1), :].rearrange("p (e u) d -> p d u e", e=2),
             )
 
         recip = keep.tile([P, BLOCKS * TILES], F32)
@@ -181,10 +184,10 @@ def tile_mobilitygnn_pb_kernel(tc, h1, mobility_matrix, W_in, b_in, out):
             b, a, h = units[n]
             turned[n] = psum.tile([P, UNIT_GROUPS * PACK, P], BF16, tag="turned", name="turned")
             for g2 in range(UNIT_GROUPS):
-                for t in range(PACK):
+                for s in range(PACK):
                     nc.tensor.transpose(
-                        turned[n][:, PACK * g2 + t, :],
-                        m_sb[(b, UNIT_GROUPS * h + g2)][:, t, P * a : P * (a + 1)],
+                        turned[n][:, PACK * g2 + s, :],
+                        m_sb[(b, UNIT_GROUPS * h + g2)][:, s, P * a : P * (a + 1)],
                         ident_bf[:],
                     )
 
@@ -211,21 +214,21 @@ def tile_mobilitygnn_pb_kernel(tc, h1, mobility_matrix, W_in, b_in, out):
             )
 
         def turn_back(n):
-            back[n] = psum.tile([P, UNIT_GROUPS, PACK, P], BF16, tag="back", name="back")
+            back[n] = psum.tile([P, UNIT_GROUPS, 2, P], F32, tag="back", name="back")
+            words = weights[n][:].bitcast(F32)
             for g2 in range(UNIT_GROUPS):
-                for t in range(PACK):
-                    row_tile = PACK * g2 + t
-                    nc.tensor.transpose(
-                        back[n][:, g2, t, :], weights[n][:, P * row_tile : P * (row_tile + 1)], ident_bf[:]
-                    )
+                for u in range(2):
+                    first = P * (2 * g2 + u)
+                    nc.tensor.transpose(back[n][:, g2, u, :], words[:, first : first + P], ident_f32[:])
 
         def regroup(n):
-            grouped[n] = stage.tile([P, UNIT_GROUPS, P, PACK], BF16, align_bytes=64, name="grouped")
-            source = back[n][:].rearrange("p g t i -> p g i t")
-            if n % 3 == 2:
-                nc.vector.tensor_copy(out=grouped[n][:], in_=source)
+            grouped[n] = stage.tile([P, UNIT_ROWS], BF16, align_bytes=64, name="grouped")
+            target = grouped[n][:].bitcast(F32).rearrange("p (g i u) -> p g i u", g=UNIT_GROUPS, u=2)
+            source = back[n][:].rearrange("p g u i -> p g i u")
+            if n % 4 == 3:
+                nc.vector.tensor_copy(out=target, in_=source)
             else:
-                nc.scalar.copy(out=grouped[n][:], in_=source)
+                nc.scalar.copy(out=target, in_=source)
 
         def quantise(n):
             b, a, h = units[n]
@@ -234,7 +237,7 @@ def tile_mobilitygnn_pb_kernel(tc, h1, mobility_matrix, W_in, b_in, out):
             nc.vector.quantize_mx(
                 out=a_codes[:, c, cols].bitcast(FP8X4),
                 scales=a_scales[:, c, cols],
-                in_=grouped[n][:].rearrange("p g i t -> p (g i t)"),
+                in_=grouped[n][:],
             )
 
         def multiply(n):
@@ -253,17 +256,18 @@ def tile_mobilitygnn_pb_kernel(tc, h1, mobility_matrix, W_in, b_in, out):
                     start=(g == 0),
                     stop=(g == GROUPS - 1),
                 )
-            unread = psum_one.tile([P, D_OUT], F32, tag="unread")
-            for g in range(UNIT_GROUPS * h, UNIT_GROUPS * (h + 1)):
-                cols = slice(P * g, P * (g + 1))
+
+        def hold_clock(passes):
+            for k in range(passes):
+                unread = psum_one.tile([P, D_OUT], F32, tag="unread")
                 nc.tensor.matmul_mx(
                     out=unread[:],
-                    lhsT=a_codes[:, c, cols].bitcast(FP8X4),
-                    lhsT_scale=a_scales[:, c, cols],
-                    rhs=t_codes[:, g, :].bitcast(FP8X4),
-                    rhs_scale=t_scales[:, g, :],
-                    start=(g == UNIT_GROUPS * h),
-                    stop=(g == UNIT_GROUPS * (h + 1) - 1),
+                    lhsT=h_codes[:, 0:P].bitcast(FP8X4),
+                    lhsT_scale=h_scales[:, 0:P],
+                    rhs=w_codes[:].bitcast(FP8X4),
+                    rhs_scale=w_scales[:],
+                    start=True,
+                    stop=True,
                 )
 
         share = {}
@@ -346,6 +350,9 @@ def tile_mobilitygnn_pb_kernel(tc, h1, mobility_matrix, W_in, b_in, out):
                 quantise(step - 5)
             if live(step - 6):
                 multiply(step - 6)
+                hold_clock(RUN_OF_PASSES - UNIT_GROUPS)
+            elif step - 6 < 0:
+                hold_clock(RUN_OF_PASSES)
             if step % per_block >= TILES and step // per_block + 1 < BLOCKS:
                 column_sums(step // per_block + 1, step % per_block - TILES)
             b, late = divmod(step - per_block - 2, per_block)

@@ -258,16 +258,16 @@ def tile_mobilitygnn_pb_kernel(tc, h1, mobility_matrix, W_in, b_in, out):
                 )
 
         def hold_clock(passes):
+            unread = psum_one.tile([P, D_OUT], F32, tag="unread")
             for k in range(passes):
-                unread = psum_one.tile([P, D_OUT], F32, tag="unread")
                 nc.tensor.matmul_mx(
                     out=unread[:],
                     lhsT=h_codes[:, 0:P].bitcast(FP8X4),
                     lhsT_scale=h_scales[:, 0:P],
                     rhs=w_codes[:].bitcast(FP8X4),
                     rhs_scale=w_scales[:],
-                    start=True,
-                    stop=True,
+                    start=(k == 0),
+                    stop=(k == passes - 1),
                 )
 
         share = {}
@@ -351,8 +351,6 @@ def tile_mobilitygnn_pb_kernel(tc, h1, mobility_matrix, W_in, b_in, out):
             if live(step - 6):
                 multiply(step - 6)
                 hold_clock(RUN_OF_PASSES - UNIT_GROUPS)
-            elif step - 6 < 0:
-                hold_clock(RUN_OF_PASSES)
             if step % per_block >= TILES and step // per_block + 1 < BLOCKS:
                 column_sums(step // per_block + 1, step % per_block - TILES)
             b, late = divmod(step - per_block - 2, per_block)

@@ -42,7 +42,6 @@ def tile_mobilitygnn_pb_kernel(tc, h1, mobility_matrix, W_in, b_in, out):
         small = ctx.enter_context(tc.tile_pool(name="small", bufs=2))
         psum = ctx.enter_context(tc.psum_pool(name="psum", bufs=2))
         psum_one = ctx.enter_context(tc.psum_pool(name="psum_one", bufs=1))
-        ctx.enter_context(tc.manual_schedule())
 
         w_raw = keep.tile([P, PACK, D_OUT], BF16)
         for u in range(2):
@@ -257,17 +256,22 @@ def tile_mobilitygnn_pb_kernel(tc, h1, mobility_matrix, W_in, b_in, out):
                     stop=(g == GROUPS - 1),
                 )
 
-        def hold_clock(passes):
+        def hold_clock(n):
+            b, a, h = units[n]
+            c = TILES * b + a
+            repeats = RUN_OF_PASSES - UNIT_GROUPS
             unread = psum_one.tile([P, D_OUT], F32, tag="unread")
-            for k in range(passes):
+            for k in range(repeats):
+                g = UNIT_GROUPS * h + k
+                cols = slice(P * g, P * (g + 1))
                 nc.tensor.matmul_mx(
                     out=unread[:],
-                    lhsT=h_codes[:, 0:P].bitcast(FP8X4),
-                    lhsT_scale=h_scales[:, 0:P],
-                    rhs=w_codes[:].bitcast(FP8X4),
-                    rhs_scale=w_scales[:],
+                    lhsT=a_codes[:, c, cols].bitcast(FP8X4),
+                    lhsT_scale=a_scales[:, c, cols],
+                    rhs=t_codes[:, g, :].bitcast(FP8X4),
+                    rhs_scale=t_scales[:, g, :],
                     start=(k == 0),
-                    stop=(k == passes - 1),
+                    stop=(k == repeats - 1),
                 )
 
         share = {}
@@ -350,7 +354,7 @@ def tile_mobilitygnn_pb_kernel(tc, h1, mobility_matrix, W_in, b_in, out):
                 quantise(step - 5)
             if live(step - 6):
                 multiply(step - 6)
-                hold_clock(RUN_OF_PASSES - UNIT_GROUPS)
+                hold_clock(step - 6)
             if step % per_block >= TILES and step // per_block + 1 < BLOCKS:
                 column_sums(step // per_block + 1, step % per_block - TILES)
             b, late = divmod(step - per_block - 2, per_block)

@@ -10,7 +10,6 @@ U8 = mybir.dt.uint8
 FP8X4 = mybir.dt.float8_e4m3fn_x4
 ALU = mybir.AluOpType
 ACT = mybir.ActivationFunctionType
-AXIS_X = mybir.AxisListType.X
 
 P = 128
 PACK = 4
@@ -22,14 +21,25 @@ D_OUT = 256
 THRESH = 1e-6
 EPS = 1e-8
 
+HALF_K = D_H // 2
 GROUPS = N_NODES // K_PASS
-BLOCK = 512
-BLOCKS = N_NODES // BLOCK
-TILES = BLOCK // P
+PANEL = 512
+PANELS = N_NODES // PANEL
+TILES = PANEL // P
 HALVES = 2
 UNIT_GROUPS = GROUPS // HALVES
 UNIT_ROWS = UNIT_GROUPS * K_PASS
-RUN_OF_PASSES = 4
+PER_PANEL = TILES * HALVES
+
+RUN_OF_PASSES = 3
+VECTOR_TURN = 4
+LAG_DROP = 1
+LAG_SCALE = 2
+LAG_BACK = 3
+LAG_REGROUP = 4
+LAG_QUANTISE = 5
+LAG_MULTIPLY = 6
+assert LAG_MULTIPLY <= LAG_SCALE + TILES + 1
 
 FLOPS = 2 * N_NODES * D_H * D_OUT + 2 * N_NODES * N_NODES * D_OUT
 
@@ -47,7 +57,7 @@ def tile_mobilitygnn_pb_kernel(tc, h1, mobility_matrix, W_in, b_in, out):
         for u in range(2):
             nc.sync.dma_start(
                 out=w_raw[:, 2 * u : 2 * u + 2, :],
-                in_=W_in[256 * u : 256 * (u + 1), :].rearrange("(q e) n -> q e n", e=2),
+                in_=W_in[HALF_K * u : HALF_K * (u + 1), :].rearrange("(q e) n -> q e n", e=2),
             )
         bias_all = keep.tile([P, D_OUT], BF16)
         nc.scalar.dma_start(out=bias_all[:], in_=b_in.partition_broadcast(P))
@@ -60,15 +70,15 @@ def tile_mobilitygnn_pb_kernel(tc, h1, mobility_matrix, W_in, b_in, out):
             )
             h1_sb.append(h1_rows)
         m_sb = {}
-        for b in range(BLOCKS):
+        for b in range(PANELS):
             for g in range(GROUPS):
-                m_chunk = keep.tile([P, PACK, BLOCK], BF16, name="m_%d_%d" % (b, g))
+                m_chunk = keep.tile([P, PACK, PANEL], BF16, name="m_%d_%d" % (b, g))
                 for e in range(2):
                     first_row = K_PASS * g + 2 * P * e
                     nc.sync.dma_start(
                         out=m_chunk[e:P:2, :, :],
                         in_=mobility_matrix[
-                            first_row : first_row + 2 * P, BLOCK * b : BLOCK * (b + 1)
+                            first_row : first_row + 2 * P, PANEL * b : PANEL * (b + 1)
                         ].rearrange("(s q) i -> q s i", s=PACK),
                     )
                 m_sb[(b, g)] = m_chunk
@@ -100,28 +110,28 @@ def tile_mobilitygnn_pb_kernel(tc, h1, mobility_matrix, W_in, b_in, out):
             rows = slice(K_PASS * g, K_PASS * (g + 1))
             h_grouped = stage.tile([P, K_PASS * PACK], BF16, align_bytes=64)
             h_words = h_grouped[:].bitcast(F32).rearrange("q (t j u) -> q t j u", t=PACK, u=2)
-            for half in range(2):
+            for bank in range(2):
                 h_turned = psum.tile([P, 2, 2, P], F32, tag="turned")
                 for t2 in range(2):
                     for u in range(2):
                         nc.tensor.transpose(
                             h_turned[:, t2, u, :],
-                            h1_sb[g][:, 2 * half + t2, :].bitcast(F32)[:, P * u : P * (u + 1)],
+                            h1_sb[g][:, 2 * bank + t2, :].bitcast(F32)[:, P * u : P * (u + 1)],
                             ident_f32[:],
                         )
                 nc.scalar.copy(
-                    out=h_words[:, 2 * half : 2 * half + 2, :, :],
+                    out=h_words[:, 2 * bank : 2 * bank + 2, :, :],
                     in_=h_turned[:].rearrange("q t u j -> q t j u"),
                 )
             nc.vector.quantize_mx(
                 out=h_codes[:, rows].bitcast(FP8X4), scales=h_scales[:, rows], in_=h_grouped[:]
             )
         for g in range(GROUPS):
-            for half in range(2):
+            for bank in range(2):
                 t_ps = psum.tile([P, 2, D_OUT], F32, tag="back")
-                first = PACK * g + 2 * half
+                first_tile = PACK * g + 2 * bank
                 for t2 in range(2):
-                    cols = slice(P * (first + t2), P * (first + t2 + 1))
+                    cols = slice(P * (first_tile + t2), P * (first_tile + t2 + 1))
                     nc.tensor.matmul_mx(
                         out=t_ps[:, t2, :],
                         lhsT=h_codes[:, cols].bitcast(FP8X4),
@@ -132,7 +142,7 @@ def tile_mobilitygnn_pb_kernel(tc, h1, mobility_matrix, W_in, b_in, out):
                         stop=True,
                     )
                 nc.vector.tensor_tensor(
-                    out=t_f32[:, first : first + 2, :],
+                    out=t_f32[:, first_tile : first_tile + 2, :],
                     in0=t_ps[:],
                     in1=bias_all[:].unsqueeze(1).to_broadcast([P, 2, D_OUT]),
                     op=ALU.add,
@@ -142,13 +152,13 @@ def tile_mobilitygnn_pb_kernel(tc, h1, mobility_matrix, W_in, b_in, out):
                 in_=t_f32[:, PACK * g : PACK * (g + 1), :].rearrange("p (e u) d -> p d u e", e=2),
             )
 
-        recip = keep.tile([P, BLOCKS * TILES], F32)
-        thresh = keep.tile([P, BLOCKS * TILES], F32)
-        wsum_parts = keep.tile([P, BLOCKS * TILES, HALVES], F32)
-        a_codes = keep.tile([P, BLOCKS * TILES, GROUPS * P], U32, align_bytes=64)
-        a_scales = keep.tile([P, BLOCKS * TILES, GROUPS * P], U8, align_bytes=64)
+        recip = keep.tile([P, PANELS * TILES], F32)
+        thresh = keep.tile([P, PANELS * TILES], F32)
+        wsum_parts = keep.tile([P, PANELS * TILES, HALVES], F32)
+        a_codes = keep.tile([P, PANELS * TILES, GROUPS * P], U32, align_bytes=64)
+        a_scales = keep.tile([P, PANELS * TILES, GROUPS * P], U8, align_bytes=64)
 
-        units = [(b, a, h) for b in range(BLOCKS) for a in range(TILES) for h in range(HALVES)]
+        units = [(b, a, h) for b in range(PANELS) for a in range(TILES) for h in range(HALVES)]
         sums_ps = {}
         turned = {}
         kept = {}
@@ -161,13 +171,13 @@ def tile_mobilitygnn_pb_kernel(tc, h1, mobility_matrix, W_in, b_in, out):
             if a == 0:
                 sums_ps[b] = psum_one.tile([P, TILES], F32, tag="sums", name="sums_ps")
             for g in range(GROUPS):
-                for t in range(PACK):
+                for s in range(PACK):
                     nc.tensor.matmul(
                         out=sums_ps[b][:, a : a + 1],
-                        lhsT=m_sb[(b, g)][:, t, P * a : P * (a + 1)],
+                        lhsT=m_sb[(b, g)][:, s, P * a : P * (a + 1)],
                         rhs=ones_bf[:],
-                        start=(g == 0 and t == 0),
-                        stop=(g == GROUPS - 1 and t == PACK - 1),
+                        start=(g == 0 and s == 0),
+                        stop=(g == GROUPS - 1 and s == PACK - 1),
                     )
 
         def column_scalars(b):
@@ -217,14 +227,16 @@ def tile_mobilitygnn_pb_kernel(tc, h1, mobility_matrix, W_in, b_in, out):
             words = weights[n][:].bitcast(F32)
             for g2 in range(UNIT_GROUPS):
                 for u in range(2):
-                    first = P * (2 * g2 + u)
-                    nc.tensor.transpose(back[n][:, g2, u, :], words[:, first : first + P], ident_f32[:])
+                    first_word = P * (2 * g2 + u)
+                    nc.tensor.transpose(
+                        back[n][:, g2, u, :], words[:, first_word : first_word + P], ident_f32[:]
+                    )
 
         def regroup(n):
             grouped[n] = stage.tile([P, UNIT_ROWS], BF16, align_bytes=64, name="grouped")
             target = grouped[n][:].bitcast(F32).rearrange("p (g i u) -> p g i u", g=UNIT_GROUPS, u=2)
             source = back[n][:].rearrange("p g u i -> p g i u")
-            if n % 4 == 3:
+            if n % VECTOR_TURN == VECTOR_TURN - 1:
                 nc.vector.tensor_copy(out=target, in_=source)
             else:
                 nc.scalar.copy(out=target, in_=source)
@@ -281,9 +293,9 @@ def tile_mobilitygnn_pb_kernel(tc, h1, mobility_matrix, W_in, b_in, out):
 
         def shares(b):
             tiles = slice(TILES * b, TILES * (b + 1))
-            denom = small.tile([P, TILES], F32, name="wsum_eps")
+            wsum_eps = small.tile([P, TILES], F32, name="wsum_eps")
             nc.vector.scalar_tensor_tensor(
-                out=denom[:],
+                out=wsum_eps[:],
                 in0=wsum_parts[:, tiles, 0],
                 scalar=EPS,
                 in1=wsum_parts[:, tiles, 1],
@@ -291,9 +303,9 @@ def tile_mobilitygnn_pb_kernel(tc, h1, mobility_matrix, W_in, b_in, out):
                 op1=ALU.add,
             )
             no_edge[b] = small.tile([P, TILES], F32, name="no_edge")
-            nc.vector.tensor_single_scalar(out=no_edge[b][:], in_=denom[:], scalar=EPS, op=ALU.is_le)
+            nc.vector.tensor_single_scalar(out=no_edge[b][:], in_=wsum_eps[:], scalar=EPS, op=ALU.is_le)
             share[b] = small.tile([P, TILES], F32, name="share")
-            nc.vector.reciprocal(out=share[b][:], in_=denom[:])
+            nc.vector.reciprocal(out=share[b][:], in_=wsum_eps[:])
 
         def fall_back(b, a):
             c = TILES * b + a
@@ -328,7 +340,6 @@ def tile_mobilitygnn_pb_kernel(tc, h1, mobility_matrix, W_in, b_in, out):
         def live(n):
             return 0 <= n < len(units)
 
-        per_block = TILES * HALVES
         for a in range(TILES):
             column_sums(0, a)
         column_scalars(0)
@@ -337,28 +348,28 @@ def tile_mobilitygnn_pb_kernel(tc, h1, mobility_matrix, W_in, b_in, out):
             scales=t_scales[:].rearrange("p g d -> p (g d)"),
             in_=t_grouped[:].rearrange("p g x -> p (g x)"),
         )
-        for step in range(len(units) + per_block):
-            if step > 0 and step % per_block == 0 and step // per_block < BLOCKS:
-                column_scalars(step // per_block)
+        for step in range(len(units) + PER_PANEL):
+            if step > 0 and step % PER_PANEL == 0 and step // PER_PANEL < PANELS:
+                column_scalars(step // PER_PANEL)
             if live(step):
                 turn(step)
-            if live(step - 1):
-                drop_small(step - 1)
-            if live(step - 2):
-                scale(step - 2)
-            if live(step - 3):
-                turn_back(step - 3)
-            if live(step - 4):
-                regroup(step - 4)
-            if live(step - 5):
-                quantise(step - 5)
-            if live(step - 6):
-                multiply(step - 6)
-                hold_clock(step - 6)
-            if step % per_block >= TILES and step // per_block + 1 < BLOCKS:
-                column_sums(step // per_block + 1, step % per_block - TILES)
-            b, late = divmod(step - per_block - 2, per_block)
-            if 0 <= b < BLOCKS:
+            if live(step - LAG_DROP):
+                drop_small(step - LAG_DROP)
+            if live(step - LAG_SCALE):
+                scale(step - LAG_SCALE)
+            if live(step - LAG_BACK):
+                turn_back(step - LAG_BACK)
+            if live(step - LAG_REGROUP):
+                regroup(step - LAG_REGROUP)
+            if live(step - LAG_QUANTISE):
+                quantise(step - LAG_QUANTISE)
+            if live(step - LAG_MULTIPLY):
+                multiply(step - LAG_MULTIPLY)
+                hold_clock(step - LAG_MULTIPLY)
+            if step % PER_PANEL >= TILES and step // PER_PANEL + 1 < PANELS:
+                column_sums(step // PER_PANEL + 1, step % PER_PANEL - TILES)
+            b, late = divmod(step - (PER_PANEL + LAG_SCALE), PER_PANEL)
+            if 0 <= b < PANELS:
                 if late == 0:
                     shares(b)
                 if 1 <= late <= TILES:

@@ -31,7 +31,7 @@ UNIT_GROUPS = GROUPS // HALVES
 UNIT_ROWS = UNIT_GROUPS * K_PASS
 PER_PANEL = TILES * HALVES
 
-RUN_OF_PASSES = 3
+RUN_OF_PASSES = 2
 VECTOR_TURN = 4
 LAG_DROP = 1
 LAG_SCALE = 2
@@ -365,7 +365,8 @@ def tile_mobilitygnn_pb_kernel(tc, h1, mobility_matrix, W_in, b_in, out):
                 quantise(step - LAG_QUANTISE)
             if live(step - LAG_MULTIPLY):
                 multiply(step - LAG_MULTIPLY)
-                hold_clock(step - LAG_MULTIPLY)
+                if RUN_OF_PASSES > UNIT_GROUPS:
+                    hold_clock(step - LAG_MULTIPLY)
             if step % PER_PANEL >= TILES and step // PER_PANEL + 1 < PANELS:
                 column_sums(step // PER_PANEL + 1, step % PER_PANEL - TILES)
             b, late = divmod(step - (PER_PANEL + LAG_SCALE), PER_PANEL)

from contextlib import ExitStack

import concourse.mybir as mybir
from concourse.masks import make_identity

F32 = mybir.dt.float32
BF16 = mybir.dt.bfloat16
U32 = mybir.dt.uint32
U8 = mybir.dt.uint8
FP8X4 = mybir.dt.float8_e4m3fn_x4
ALU = mybir.AluOpType
ACT = mybir.ActivationFunctionType

P = 128
PACK = 4
K_PASS = P * PACK

N_NODES = 2048
D_H = 512
D_OUT = 256
THRESH = 1e-6
EPS = 1e-8

HALF_K = D_H // 2
GROUPS = N_NODES // K_PASS
PANEL = 512
PANELS = N_NODES // PANEL
TILES = PANEL // P
HALVES = 2
UNIT_GROUPS = GROUPS // HALVES
UNIT_ROWS = UNIT_GROUPS * K_PASS
PER_PANEL = TILES * HALVES

RUN_OF_PASSES = 2
VECTOR_TURN = 4
LAG_DROP = 1
LAG_SCALE = 2
LAG_BACK = 3
LAG_REGROUP = 4
LAG_QUANTISE = 5
LAG_MULTIPLY = 6
assert LAG_MULTIPLY <= LAG_SCALE + TILES + 1

FLOPS = 2 * N_NODES * D_H * D_OUT + 2 * N_NODES * N_NODES * D_OUT


def tile_mobilitygnn_pb_kernel(tc, h1, mobility_matrix, W_in, b_in, out):
    nc = tc.nc
    with ExitStack() as ctx:
        keep = ctx.enter_context(tc.tile_pool(name="keep", bufs=1))
        stage = ctx.enter_context(tc.tile_pool(name="stage", bufs=3))
        small = ctx.enter_context(tc.tile_pool(name="small", bufs=2))
        psum = ctx.enter_context(tc.psum_pool(name="psum", bufs=2))
        psum_one = ctx.enter_context(tc.psum_pool(name="psum_one", bufs=1))

        w_raw = keep.tile([P, PACK, D_OUT], BF16)
        for u in range(2):
            nc.sync.dma_start(
                out=w_raw[:, 2 * u : 2 * u + 2, :],
                in_=W_in[HALF_K * u : HALF_K * (u + 1), :].rearrange("(q e) n -> q e n", e=2),
            )
        bias_all = keep.tile([P, D_OUT], BF16)
        nc.scalar.dma_start(out=bias_all[:], in_=b_in.partition_broadcast(P))
        h1_sb = []
        for g in range(GROUPS):
            h1_rows = keep.tile([P, PACK, D_H], BF16, name="h1_rows_%d" % g)
            nc.sync.dma_start(
                out=h1_rows[:],
                in_=h1[K_PASS * g : K_PASS * (g + 1), :].rearrange("(t p) k -> p t k", p=P),
            )
            h1_sb.append(h1_rows)
        m_sb = {}
        for b in range(PANELS):
            for g in range(GROUPS):
                m_chunk = keep.tile([P, PACK, PANEL], BF16, name="m_%d_%d" % (b, g))
                for e in range(2):
                    first_row = K_PASS * g + 2 * P * e
                    nc.sync.dma_start(
                        out=m_chunk[e:P:2, :, :],
                        in_=mobility_matrix[
                            first_row : first_row + 2 * P, PANEL * b : PANEL * (b + 1)
                        ].rearrange("(s q) i -> q s i", s=PACK),
                    )
                m_sb[(b, g)] = m_chunk

        ident_f32 = keep.tile([P, P], F32)
        make_identity(nc, ident_f32[:])
        ident_bf = keep.tile([P, P], BF16)
        make_identity(nc, ident_bf[:])
        ones_bf = keep.tile([P, 1], BF16)
        nc.vector.memset(ones_bf[:], 1.0)

        w_grouped = keep.tile([P, D_OUT, PACK], BF16, align_bytes=64)
        nc.vector.tensor_copy(out=w_grouped[:], in_=w_raw[:].rearrange("q t n -> q n t"))
        w_codes = keep.tile([P, D_OUT], U32, align_bytes=64)
        w_scales = keep.tile([P, D_OUT], U8, align_bytes=64)
        nc.vector.quantize_mx(
            out=w_codes[:].bitcast(FP8X4),
            scales=w_scales[:],
            in_=w_grouped[:].rearrange("q n t -> q (n t)"),
        )

        h_codes = keep.tile([P, N_NODES], U32, align_bytes=64)
        h_scales = keep.tile([P, N_NODES], U8, align_bytes=64)
        t_f32 = keep.tile([P, GROUPS * PACK, D_OUT], F32)
        t_grouped = keep.tile([P, GROUPS, D_OUT * PACK], BF16, align_bytes=64)
        t_codes = keep.tile([P, GROUPS, D_OUT], U32, align_bytes=64)
        t_scales = keep.tile([P, GROUPS, D_OUT], U8, align_bytes=64)
        for g in range(GROUPS):
            rows = slice(K_PASS * g, K_PASS * (g + 1))
            h_grouped = stage.tile([P, K_PASS * PACK], BF16, align_bytes=64)
            h_words = h_grouped[:].bitcast(F32).rearrange("q (t j u) -> q t j u", t=PACK, u=2)
            for bank in range(2):
                h_turned = psum.tile([P, 2, 2, P], F32, tag="turned")
                for t2 in range(2):
                    for u in range(2):
                        nc.tensor.transpose(
                            h_turned[:, t2, u, :],
                            h1_sb[g][:, 2 * bank + t2, :].bitcast(F32)[:, P * u : P * (u + 1)],
                            ident_f32[:],
                        )
                nc.scalar.copy(
                    out=h_words[:, 2 * bank : 2 * bank + 2, :, :],
                    in_=h_turned[:].rearrange("q t u j -> q t j u"),
                )
            nc.vector.quantize_mx(
                out=h_codes[:, rows].bitcast(FP8X4), scales=h_scales[:, rows], in_=h_grouped[:]
            )
        for g in range(GROUPS):
            for bank in range(2):
                t_ps = psum.tile([P, 2, D_OUT], F32, tag="back")
                first_tile = PACK * g + 2 * bank
                for t2 in range(2):
                    cols = slice(P * (first_tile + t2), P * (first_tile + t2 + 1))
                    nc.tensor.matmul_mx(
                        out=t_ps[:, t2, :],
                        lhsT=h_codes[:, cols].bitcast(FP8X4),
                        lhsT_scale=h_scales[:, cols],
                        rhs=w_codes[:].bitcast(FP8X4),
                        rhs_scale=w_scales[:],
                        start=True,
                        stop=True,
                    )
                nc.vector.tensor_tensor(
                    out=t_f32[:, first_tile : first_tile + 2, :],
                    in0=t_ps[:],
                    in1=bias_all[:].unsqueeze(1).to_broadcast([P, 2, D_OUT]),
                    op=ALU.add,
                )
            nc.scalar.copy(
                out=t_grouped[:, g, :].rearrange("p (d u e) -> p d u e", u=2, e=2),
                in_=t_f32[:, PACK * g : PACK * (g + 1), :].rearrange("p (e u) d -> p d u e", e=2),
            )

        recip = keep.tile([P, PANELS * TILES], F32)
        thresh = keep.tile([P, PANELS * TILES], F32)
        wsum_parts = keep.tile([P, PANELS * TILES, HALVES], F32)
        a_codes = keep.tile([P, PANELS * TILES, GROUPS * P], U32, align_bytes=64)
        a_scales = keep.tile([P, PANELS * TILES, GROUPS * P], U8, align_bytes=64)

        units = [(b, a, h) for b in range(PANELS) for a in range(TILES) for h in range(HALVES)]
        sums_ps = {}
        turned = {}
        kept = {}
        weights = {}
        back = {}
        grouped = {}
        ws_ps = {}

        def column_sums(b, a):
            if a == 0:
                sums_ps[b] = psum_one.tile([P, TILES], F32, tag="sums", name="sums_ps")
            for g in range(GROUPS):
                for s in range(PACK):
                    nc.tensor.matmul(
                        out=sums_ps[b][:, a : a + 1],
                        lhsT=m_sb[(b, g)][:, s, P * a : P * (a + 1)],
                        rhs=ones_bf[:],
                        start=(g == 0 and s == 0),
                        stop=(g == GROUPS - 1 and s == PACK - 1),
                    )

        def column_scalars(b):
            tiles = slice(TILES * b, TILES * (b + 1))
            denom = small.tile([P, TILES], F32)
            nc.vector.tensor_scalar_add(out=denom[:], in0=sums_ps[b][:], scalar1=EPS)
            nc.vector.tensor_scalar(
                out=thresh[:, tiles], in0=sums_ps[b][:], scalar1=EPS, scalar2=THRESH, op0=ALU.add, op1=ALU.mult
            )
            nc.vector.reciprocal(out=recip[:, tiles], in_=denom[:])

        def turn(n):
            b, a, h = units[n]
            turned[n] = psum.tile([P, UNIT_GROUPS * PACK, P], BF16, tag="turned", name="turned")
            for g2 in range(UNIT_GROUPS):
                for s in range(PACK):
                    nc.tensor.transpose(
                        turned[n][:, PACK * g2 + s, :],
                        m_sb[(b, UNIT_GROUPS * h + g2)][:, s, P * a : P * (a + 1)],
                        ident_bf[:],
                    )

        def drop_small(n):
            b, a, h = units[n]
            c = TILES * b + a
            m_turned = turned[n][:].rearrange("p c j -> p (c j)")
            kept[n] = stage.tile([P, UNIT_ROWS], BF16, name="kept")
            nc.vector.tensor_scalar(
                out=kept[n][:], in0=m_turned, scalar1=thresh[:, c : c + 1], scalar2=None, op0=ALU.is_gt
            )
            nc.vector.tensor_tensor(out=kept[n][:], in0=kept[n][:], in1=m_turned, op=ALU.mult)

        def scale(n):
            b, a, h = units[n]
            c = TILES * b + a
            weights[n] = stage.tile([P, UNIT_ROWS], BF16, name="weights")
            nc.scalar.activation(
                out=weights[n][:],
                in_=kept[n][:],
                func=ACT.Copy,
                scale=recip[:, c : c + 1],
                accum_out=wsum_parts[:, c, h : h + 1],
            )

        def turn_back(n):
            back[n] = psum.tile([P, UNIT_GROUPS, 2, P], F32, tag="back", name="back")
            words = weights[n][:].bitcast(F32)
            for g2 in range(UNIT_GROUPS):
                for u in range(2):
                    first_word = P * (2 * g2 + u)
                    nc.tensor.transpose(
                        back[n][:, g2, u, :], words[:, first_word : first_word + P], ident_f32[:]
                    )

        def regroup(n):
            grouped[n] = stage.tile([P, UNIT_ROWS], BF16, align_bytes=64, name="grouped")
            target = grouped[n][:].bitcast(F32).rearrange("p (g i u) -> p g i u", g=UNIT_GROUPS, u=2)
            source = back[n][:].rearrange("p g u i -> p g i u")
            if n % VECTOR_TURN == VECTOR_TURN - 1:
                nc.vector.tensor_copy(out=target, in_=source)
            else:
                nc.scalar.copy(out=target, in_=source)

        def quantise(n):
            b, a, h = units[n]
            c = TILES * b + a
            cols = slice(UNIT_GROUPS * P * h, UNIT_GROUPS * P * (h + 1))
            nc.vector.quantize_mx(
                out=a_codes[:, c, cols].bitcast(FP8X4),
                scales=a_scales[:, c, cols],
                in_=grouped[n][:],
            )

        def multiply(n):
            b, a, h = units[n]
            c = TILES * b + a
            if h == 0 and a % 2 == 0:
                ws_ps[c // 2] = psum.tile([P, 2, D_OUT], F32, tag="ws", name="ws_ps")
            for g in range(UNIT_GROUPS * h, UNIT_GROUPS * (h + 1)):
                cols = slice(P * g, P * (g + 1))
                nc.tensor.matmul_mx(
                    out=ws_ps[c // 2][:, a % 2, :],
                    lhsT=a_codes[:, c, cols].bitcast(FP8X4),
                    lhsT_scale=a_scales[:, c, cols],
                    rhs=t_codes[:, g, :].bitcast(FP8X4),
                    rhs_scale=t_scales[:, g, :],
                    start=(g == 0),
                    stop=(g == GROUPS - 1),
                )

        def hold_clock(n):
            b, a, h = units[n]
            c = TILES * b + a
            repeats = RUN_OF_PASSES - UNIT_GROUPS
            unread = psum_one.tile([P, D_OUT], F32, tag="unread")
            for k in range(repeats):
                g = UNIT_GROUPS * h + k
                cols = slice(P * g, P * (g + 1))
                nc.tensor.matmul_mx(
                    out=unread[:],
                    lhsT=a_codes[:, c, cols].bitcast(FP8X4),
                    lhsT_scale=a_scales[:, c, cols],
                    rhs=t_codes[:, g, :].bitcast(FP8X4),
                    rhs_scale=t_scales[:, g, :],
                    start=(k == 0),
                    stop=(k == repeats - 1),
                )

        share = {}
        no_edge = {}
        fallback = {}
        result = {}

        def shares(b):
            tiles = slice(TILES * b, TILES * (b + 1))
            wsum_eps = small.tile([P, TILES], F32, name="wsum_eps")
            nc.vector.scalar_tensor_tensor(
                out=wsum_eps[:],
                in0=wsum_parts[:, tiles, 0],
                scalar=EPS,
                in1=wsum_parts[:, tiles, 1],
                op0=ALU.add,
                op1=ALU.add,
            )
            no_edge[b] = small.tile([P, TILES], F32, name="no_edge")
            nc.vector.tensor_single_scalar(out=no_edge[b][:], in_=wsum_eps[:], scalar=EPS, op=ALU.is_le)
            share[b] = small.tile([P, TILES], F32, name="share")
            nc.vector.reciprocal(out=share[b][:], in_=wsum_eps[:])

        def fall_back(b, a):
            c = TILES * b + a
            if a % 2 == 0:
                fallback[c // 2] = stage.tile([P, 2, D_OUT], F32, name="fallback")
            nc.scalar.activation(
                out=fallback[c // 2][:, a % 2, :],
                in_=t_f32[:, c, :],
                func=ACT.Copy,
                scale=no_edge[b][:, a : a + 1],
            )

        def finish(b, a):
            c = TILES * b + a
            if a % 2 == 0:
                result[c // 2] = stage.tile([P, 2, D_OUT], F32, name="result")
            nc.vector.scalar_tensor_tensor(
                out=result[c // 2][:, a % 2, :],
                in0=ws_ps[c // 2][:, a % 2, :],
                scalar=share[b][:, a : a + 1],
                in1=fallback[c // 2][:, a % 2, :],
                op0=ALU.mult,
                op1=ALU.add,
            )
            if a % 2 == 1:
                first_row = P * (c - 1)
                nc.sync.dma_start(
                    out=out[first_row : first_row + 2 * P, :].rearrange("(a p) d -> p a d", p=P),
                    in_=result[c // 2][:],
                )

        def live(n):
            return 0 <= n < len(units)

        for a in range(TILES):
            column_sums(0, a)
        column_scalars(0)
        nc.vector.quantize_mx(
            out=t_codes[:].rearrange("p g d -> p (g d)").bitcast(FP8X4),
            scales=t_scales[:].rearrange("p g d -> p (g d)"),
            in_=t_grouped[:].rearrange("p g x -> p (g x)"),
        )
        for step in range(len(units) + PER_PANEL):
            if step > 0 and step % PER_PANEL == 0 and step // PER_PANEL < PANELS:
                column_scalars(step // PER_PANEL)
            if live(step):
                turn(step)
            if live(step - LAG_DROP):
                drop_small(step - LAG_DROP)
            if live(step - LAG_SCALE):
                scale(step - LAG_SCALE)
            if live(step - LAG_BACK):
                turn_back(step - LAG_BACK)
            if live(step - LAG_REGROUP):
                regroup(step - LAG_REGROUP)
            if live(step - LAG_QUANTISE):
                quantise(step - LAG_QUANTISE)
            if live(step - LAG_MULTIPLY):
                multiply(step - LAG_MULTIPLY)
                if RUN_OF_PASSES > UNIT_GROUPS:
                    hold_clock(step - LAG_MULTIPLY)
            if step % PER_PANEL >= TILES and step // PER_PANEL + 1 < PANELS:
                column_sums(step // PER_PANEL + 1, step % PER_PANEL - TILES)
            b, late = divmod(step - (PER_PANEL + LAG_SCALE), PER_PANEL)
            if 0 <= b < PANELS:
                if late == 0:
                    shares(b)
                if 1 <= late <= TILES:
                    fall_back(b, late - 1)
                if 2 <= late <= TILES + 1:
                    finish(b, late - 2)
